import numpy as np
import ml_dtypes


def mxq(x, axis, fmt="e4m3"):
    dtype, down = {"e4m3": (ml_dtypes.float8_e4m3fn, 7), "e5m2": (ml_dtypes.float8_e5m2, 14)}[fmt]
    v = np.moveaxis(np.asarray(x, np.float32).astype(ml_dtypes.bfloat16).astype(np.float64), axis, -1)
    blocks = v.reshape(v.shape[:-1] + (-1, 32))
    amax = np.abs(blocks).max(-1, keepdims=True)
    byte = np.maximum(np.where(amax > 0, np.frexp(amax)[1] - 1 + 127, 0) - down, 1)
    scale = np.exp2(byte - 127.0)
    codes = (blocks / scale).astype(np.float32).astype(dtype).astype(np.float64)
    return np.moveaxis((codes * scale).reshape(v.shape), -1, axis)


WIDE = False


def mx_kscale(k):
    if not WIDE:
        return np.ones(k)
    levels = np.array([18, -18])
    if k % 512:
        return np.exp2(np.random.permutation(np.resize(levels, k // 32))).repeat(32)
    a = np.empty((k // 512, 16))
    for p in range(k // 512):
        a[p, :8] = np.random.permutation(np.resize(levels, 8))
        for g in range(8):
            far = levels[np.abs(levels - a[p, g]) >= 10]
            a[p, g + 8] = far[np.random.randint(len(far))]
    return np.exp2(a.ravel()).repeat(32)


BF16 = ml_dtypes.bfloat16


def bf(x):
    return np.asarray(x, np.float32).astype(BF16)


def f64(x):
    return np.asarray(x).astype(np.float64)


IN_C, OUT_C, N, ND = 512, 1024, 512, 2


def sigmoid(v):
    return 1.0 / (1.0 + np.exp(-v))


def setup_inputs():
    s = mx_kscale(N)[None, :]
    u = mx_kscale(OUT_C)[:, None]
    rn = np.random.standard_normal
    x0 = bf(rn((IN_C, N)))
    h0 = bf(rn((OUT_C, N)))
    h1 = bf(rn((OUT_C, N)))
    ct0 = bf(rn((OUT_C, N)) * 0.65)
    ct1 = bf(rn((OUT_C, N)) * 0.65)
    w0 = bf(rn((OUT_C, IN_C)) * 0.7 / np.sqrt(IN_C))
    w_ho = bf(rn((OUT_C, OUT_C)) * 0.7 / np.sqrt(OUT_C))
    b_o = bf(rn((OUT_C, 1)) * 0.5)
    ws = bf(0.4 + 0.5 * np.random.random(ND))
    g = bf(16.0 * rn((OUT_C, N)) * np.exp2(np.random.randint(-6, 1, (1, N))) / s * u)
    xo = f64(w0) @ f64(x0)
    o0 = sigmoid(xo + f64(w_ho) @ f64(h0) + f64(b_o))
    o1 = sigmoid(xo + f64(w_ho) @ f64(h1) + f64(b_o))
    return {"x": bf(f64(x0) * s),
            "h_prev_dim0": h0,
            "h_prev_dim1": h1,
            "ct0": ct0,
            "ct1": ct1,
            "w_io": bf(f64(w0) / u),
            "w_ho": w_ho,
            "b_o": b_o,
            "weighted_sum": ws,
            "o_dim0": np.asarray(o0, np.float32),
            "o_dim1": np.asarray(o1, np.float32),
            "grad_out": g}


def reference(x, h_prev_dim0, h_prev_dim1, ct0, ct1, w_io, w_ho, b_o, weighted_sum, o_dim0, o_dim1, grad_out):
    ws = f64(weighted_sum)
    o0, o1 = f64(o_dim0), f64(o_dim1)
    d = ws[0] * np.tanh(f64(ct0)) * o0 * (1.0 - o0) + ws[1] * np.tanh(f64(ct1)) * o1 * (1.0 - o1)
    dz = f64(grad_out) * d
    dx = mxq(f64(w_io), 0, "e4m3").T @ mxq(dz, 0, "e5m2")
    dw = mxq(dz, 1, "e5m2") @ mxq(f64(x), 1, "e4m3").T
    return dx, dw

@@ -1,0 +1,386 @@
+from contextlib import ExitStack
+
+import concourse.mybir as mybir
+from concourse.masks import make_identity
+
+IN_C, OUT_C, N = 512, 1024, 512
+FLOPS = 2 * 2 * IN_C * OUT_C * N
+BYTES = 2 * (IN_C * N + 3 * OUT_C * N + OUT_C * IN_C + 2) + 4 * (2 * OUT_C * N + IN_C * N + OUT_C * IN_C)
+
+F32 = mybir.dt.float32
+BF16 = mybir.dt.bfloat16
+U32 = mybir.dt.uint32
+U8 = mybir.dt.uint8
+E4M3 = mybir.dt.float8_e4m3fn_x4
+E5M2 = mybir.dt.float8_e5m2_x4
+ALU = mybir.AluOpType
+ACT = mybir.ActivationFunctionType
+
+P = 128
+PACK = 4
+PASSES = OUT_C // (P * PACK)
+SLABS = PASSES * PACK
+HALF = N // 2
+LOADS = [(0, 1), (1, 1), (2, 2), (4, 2), (6, 2)]
+
+
+def tile_mdlstmcellweights_pb_v_kernel(
+    tc, x, h_prev_dim0, h_prev_dim1, ct0, ct1, w_io, w_ho, b_o, weighted_sum, o_dim0, o_dim1, grad_out, out_0, out_1
+):
+    nc = tc.nc
+
+    def slabs_of(t, s0, count):
+        g, j = divmod(s0, PACK)
+        return t.rearrange("(g p j) n -> p g j n", p=P, j=PACK)[:, g, j : j + count, :]
+
+    def by_half(ap):
+        return ap.rearrange("p (k u e) -> p u k e", u=2, e=2)
+
+    load_of = {}
+    for i, (s0, count) in enumerate(LOADS):
+        for jj in range(count):
+            load_of[s0 + jj] = (i, jj)
+
+    with ExitStack() as ctx:
+        sb = ctx.enter_context(tc.tile_pool(name="sb", bufs=1))
+        ps = ctx.enter_context(tc.psum_pool(name="ps", bufs=1))
+        ctx.enter_context(tc.manual_schedule())
+
+        ident = sb.tile([P, P], F32, name="ident")
+        make_identity(nc, ident[:])
+
+        gates, cells, grads = [], [], []
+        for i, (s0, count) in enumerate(LOADS):
+            gates.append(sb.tile([P, 2, count, N], F32, name="gates%d" % i))
+            cells.append([sb.tile([P, count, N], BF16, name="cell%d_%d" % (i, d)) for d in range(2)])
+            grads.append(sb.tile([P, count, N], BF16, name="grad%d" % i))
+        ws = sb.tile([P, 2], BF16, name="ws")
+        x_raw = sb.tile([P, PACK, N], BF16, name="x_raw")
+        w_raw = [sb.tile([P, PACK, IN_C], BF16, name="w_raw%d" % g) for g in range(PASSES)]
+
+        def load_gate(i, d):
+            nc.sync.dma_start(out=gates[i][:, d], in_=slabs_of((o_dim0, o_dim1)[d], *LOADS[i]))
+
+        def load_cell(i, d):
+            nc.sync.dma_start(out=cells[i][d][:], in_=slabs_of((ct0, ct1)[d], *LOADS[i]))
+
+        def load_grad(i):
+            nc.sync.dma_start(out=grads[i][:], in_=slabs_of(grad_out, *LOADS[i]))
+
+        def load_w(g):
+            nc.sync.dma_start(out=w_raw[g][:], in_=slabs_of(w_io, g * PACK, PACK))
+
+        load_gate(0, 0)
+        load_cell(0, 0)
+        nc.sync.dma_start(out=ws[:], in_=weighted_sum.partition_broadcast(P))
+        load_gate(0, 1)
+        load_cell(0, 1)
+        load_grad(0)
+        for i in (1, 2):
+            for d in range(2):
+                load_gate(i, d)
+            for d in range(2):
+                load_cell(i, d)
+            load_grad(i)
+        for d in range(2):
+            load_cell(3, d)
+        nc.sync.dma_start(out=x_raw[:], in_=x.rearrange("(p a) n -> p a n", a=PACK))
+        for d in range(2):
+            load_gate(3, d)
+        for d in range(2):
+            load_cell(4, d)
+        load_w(0)
+        load_grad(3)
+        for d in range(2):
+            load_gate(4, d)
+        load_grad(4)
+        load_w(1)
+
+        tanhs, grad_t, slope, term, sums, dz_pos, pos_codes = {}, {}, {}, {}, {}, {}, {}
+        back, dz_chan, chan_codes, w_packed, w_codes, dw_acc, dx_acc = {}, {}, {}, {}, {}, {}, {}
+        grad_bank, x_bank = {}, {}
+        x_packed = sb.tile([P, IN_C * PACK], BF16, name="x_packed", align_bytes=64)
+
+        def mx_tiles(name, width):
+            codes = sb.tile([P, width], U32, name=name + "_codes", align_bytes=64)
+            scales = sb.tile([P, width], U8, name=name + "_scales", align_bytes=64)
+            return codes, scales
+
+        x_codes = mx_tiles("x", IN_C)
+
+        def quantize(dst, cols, src, fmt):
+            nc.vector.quantize_mx(out=dst[0][:, cols].bitcast(fmt), scales=dst[1][:, cols], in_=src)
+
+        def tanh_of(i, d):
+            count = LOADS[i][1]
+            t = sb.tile([P, 2, count * HALF], F32, name="tanh%d_%d" % (i, d))
+            nc.scalar.activation(
+                out=t[:].rearrange("p u (k e) -> p u k e", e=2),
+                in_=by_half(cells[i][d][:].rearrange("p j n -> p (j n)")),
+                func=ACT.Tanh,
+            )
+            tanhs[i, d] = t
+
+        def turn_grad(i):
+            count = LOADS[i][1]
+            words = grads[i][:].rearrange("p j n -> p (j n)").bitcast(F32)
+            bank = ps.tile([P, count * 2, P], F32, name="grad_bank%d" % i, tag="grad")
+            for jj in range(count):
+                for u in range(2):
+                    nc.tensor.transpose(bank[:, 2 * jj + u, :], words[:, jj * HALF + u : (jj + 1) * HALF : 2], ident[:])
+            grad_bank[i] = bank
+
+        def pack_grad(i):
+            count = LOADS[i][1]
+            bank = grad_bank[i]
+            gt = sb.tile([P, count * N], BF16, name="grad_t%d" % i)
+            nc.scalar.copy(
+                out=gt[:].bitcast(F32).rearrange("p (j c u) -> p j c u", j=count, u=2),
+                in_=bank[:].rearrange("p (j u) c -> p j c u", u=2),
+            )
+            grad_t[i] = gt
+
+        def turn_x():
+            words = x_raw[:].rearrange("p a n -> p (a n)").bitcast(F32)
+            for h in range(2):
+                bank = ps.tile([P, 4, P], F32, name="x_bank%d" % h, tag="dw", bufs=2)
+                for a in range(2 * h, 2 * h + 2):
+                    for u in range(2):
+                        nc.tensor.transpose(
+                            bank[:, 2 * (a % 2) + u, :], words[:, a * HALF + u : (a + 1) * HALF : 2], ident[:]
+                        )
+                x_bank[h] = bank
+
+        def pack_x():
+            for h in range(2):
+                bank = x_bank[h]
+                nc.scalar.copy(
+                    out=x_packed[:].bitcast(F32).rearrange("q (p h k) -> q h p k", h=2, k=4)[:, h],
+                    in_=bank[:].rearrange("q k p -> q p k"),
+                )
+
+        def pack_w(g, half, copy=nc.scalar.copy):
+            if half == 0:
+                w_packed[g] = sb.tile([P, IN_C * PACK], BF16, name="w_packed%d" % g, align_bytes=64)
+            cols = slice(half * 64, half * 64 + 64)
+            copy(
+                out=w_packed[g][:].rearrange("p (c i j) -> p c j i", i=4, j=PACK)[:, cols],
+                in_=w_raw[g][:].rearrange("p j (c i) -> p c j i", i=4)[:, cols],
+            )
+
+        def quantize_w(g):
+            w_codes[g] = mx_tiles("w%d" % g, IN_C)
+            quantize(w_codes[g], slice(0, IN_C), w_packed[g][:], E4M3)
+
+        def gate_slope(i, d0, d1):
+            width = LOADS[i][1] * HALF
+            if d0 == 0:
+                slope[i] = sb.tile([P, 2, 2 * width], F32, name="slope%d" % i, tag="slope", bufs=2)
+            o = by_half(gates[i][:, d0:d1].rearrange("p d j n -> p (d j n)"))
+            for u in range(2):
+                nc.vector.scalar_tensor_tensor(
+                    out=slope[i][:, u, d0 * width : d1 * width].rearrange("p (k e) -> p k e", e=2),
+                    in0=o[:, u],
+                    scalar=1.0,
+                    in1=o[:, u],
+                    op0=ALU.subtract,
+                    op1=ALU.mult,
+                )
+
+        def direction_term(i, d):
+            s0, count = LOADS[i]
+            width = count * HALF
+            q = sb.tile([P, 2, width], F32, name="term%d_%d" % (i, d), tag="term", bufs=2)
+            nc.vector.scalar_tensor_tensor(
+                out=q[:],
+                in0=tanhs[i, d][:],
+                scalar=ws[:, d : d + 1],
+                in1=slope[i][:, :, d * width : (d + 1) * width],
+                op0=ALU.mult,
+                op1=ALU.mult,
+            )
+            for jj in range(count):
+                s = s0 + jj
+                if d == 0:
+                    sums[s] = ps.tile([P, PACK, P], F32, name="sum%d" % s, tag="sum", bufs=3)
+                for t in range(PACK):
+                    u, e = divmod(t, 2)
+                    nc.tensor.matmul(
+                        sums[s][:, t, :],
+                        lhsT=q[:, u, jj * HALF + e : (jj + 1) * HALF : 2],
+                        rhs=ident[:],
+                        is_transpose=True,
+                        start=(d == 0 and t == 0),
+                        stop=(d == 1 and t == PACK - 1),
+                    )
+
+        def round_dz(i):
+            s0, count = LOADS[i]
+            dz_pos[i] = sb.tile([P, count * N], BF16, name="dz_pos%d" % i, align_bytes=64)
+            words = dz_pos[i][:].bitcast(F32)
+            for jj in range(count):
+                cols = slice(jj * N, (jj + 1) * N)
+                nc.vector.scalar_tensor_tensor(
+                    out=dz_pos[i][:, cols].rearrange("p (c t) -> p c t", t=PACK),
+                    in0=sums[s0 + jj][:].rearrange("p t c -> p c t"),
+                    scalar=-1.0,
+                    in1=grad_t[i][:, cols].rearrange("p (c t) -> p c t", t=PACK),
+                    op0=ALU.mult,
+                    op1=ALU.mult,
+                )
+                g, j = divmod(s0 + jj, PACK)
+                for u in range(2):
+                    if j == 0:
+                        back[g, u] = ps.tile([P, PACK, P], F32, name="back%d_%d" % (g, u), tag="back%d" % u)
+                    nc.tensor.transpose(back[g, u][:, j, :], words[:, jj * HALF + u : (jj + 1) * HALF : 2], ident[:])
+
+        def quantize_pos(i):
+            width = LOADS[i][1] * P
+            pos_codes[i] = mx_tiles("pos%d" % i, width)
+            quantize(pos_codes[i], slice(0, width), dz_pos[i][:], E5M2)
+
+        def pack_chan(g, u, copy):
+            dz_chan[g, u] = sb.tile([P, HALF * PACK], BF16, name="dz_chan%d_%d" % (g, u), align_bytes=64)
+            copy(
+                out=dz_chan[g, u][:].rearrange("p (k j) -> p k j", j=PACK),
+                in_=back[g, u][:].rearrange("p j m -> p (j m)").bitcast(BF16).rearrange("p (j k) -> p k j", j=PACK),
+            )
+
+        def quantize_chan(g, u):
+            if g not in chan_codes:
+                chan_codes[g] = mx_tiles("chan%d" % g, N)
+            quantize(chan_codes[g], slice(u * HALF, (u + 1) * HALF), dz_chan[g, u][:], E5M2)
+
+        def dw_matmul(s, tag="dw", bufs=2):
+            i, jj = load_of[s]
+            cols = slice(jj * P, (jj + 1) * P)
+            dw_acc[s] = ps.tile([P, IN_C], F32, name="dw_acc%d" % s, tag=tag, bufs=bufs)
+            nc.tensor.matmul_mx(
+                out=dw_acc[s][:],
+                lhsT=pos_codes[i][0][:, cols].bitcast(E5M2),
+                lhsT_scale=pos_codes[i][1][:, cols],
+                rhs=x_codes[0][:].bitcast(E4M3),
+                rhs_scale=x_codes[1][:],
+                start=True,
+                stop=True,
+            )
+
+        def dw_store(s, copy=nc.scalar.copy):
+            res = sb.tile([P, 1, IN_C], F32, name="dw%d" % s)
+            copy(out=res[:, 0, :], in_=dw_acc[s][:])
+            nc.sync.dma_start(out=slabs_of(out_1, s, 1), in_=res[:])
+
+        def dx_matmul(a, g):
+            if g == 0:
+                tag, bufs = (("grad", 1), ("sum", 3), ("sum", 3), ("sum", 3))[a]
+                dx_acc[a] = ps.tile([P, N], F32, name="dx_acc%d" % a, tag=tag, bufs=bufs)
+            cols = slice(a * P, (a + 1) * P)
+            nc.tensor.matmul_mx(
+                out=dx_acc[a][:],
+                lhsT=w_codes[g][0][:, cols].bitcast(E4M3),
+                lhsT_scale=w_codes[g][1][:, cols],
+                rhs=chan_codes[g][0][:].bitcast(E5M2),
+                rhs_scale=chan_codes[g][1][:],
+                start=(g == 0),
+                stop=(g == PASSES - 1),
+            )
+
+        def dx_store(a, copy):
+            res = sb.tile([P, N], F32, name="dx%d" % a)
+            copy(
+                out=res[:].rearrange("p (m u e) -> p m u e", u=2, e=2),
+                in_=dx_acc[a][:].rearrange("p (u m e) -> p m u e", u=2, e=2),
+            )
+            nc.sync.dma_start(out=out_0[a * P : (a + 1) * P, :], in_=res[:])
+
+        tanh_of(0, 0)
+        gate_slope(0, 0, 1)
+        tanh_of(0, 1)
+        direction_term(0, 0)
+        gate_slope(0, 1, 2)
+        turn_grad(0)
+        pack_grad(0)
+        direction_term(0, 1)
+        tanh_of(1, 0)
+        tanh_of(1, 1)
+
+        turn_grad(1)
+        pack_grad(1)
+        gate_slope(1, 0, 2)
+        round_dz(0)
+        direction_term(1, 0)
+        quantize_pos(0)
+        direction_term(1, 1)
+        tanh_of(2, 0)
+        tanh_of(2, 1)
+
+        turn_grad(2)
+        pack_grad(2)
+        gate_slope(2, 0, 2)
+        round_dz(1)
+        tanh_of(3, 0)
+        tanh_of(3, 1)
+        turn_x()
+        pack_x()
+        direction_term(2, 0)
+        quantize_pos(1)
+        direction_term(2, 1)
+        tanh_of(4, 0)
+        tanh_of(4, 1)
+
+        gate_slope(3, 0, 2)
+        quantize(x_codes, slice(0, IN_C), x_packed[:], E4M3)
+        turn_grad(3)
+        dw_matmul(0)
+        dw_matmul(1)
+        round_dz(2)
+        pack_w(0, 0)
+        dw_store(0)
+        dw_store(1)
+        pack_grad(3)
+        pack_chan(0, 0, nc.scalar.copy)
+        pack_chan(0, 1, nc.scalar.copy)
+        direction_term(3, 0)
+        quantize_pos(2)
+        dw_matmul(2)
+        dw_matmul(3)
+        direction_term(3, 1)
+        pack_w(0, 1)
+        dw_store(2)
+        dw_store(3)
+
+        turn_grad(4)
+        pack_grad(4)
+        gate_slope(4, 0, 2)
+        round_dz(3)
+        pack_w(1, 0)
+        quantize_w(0)
+        quantize_pos(3)
+        dw_matmul(4)
+        dw_matmul(5)
+        dw_store(4)
+        dw_store(5)
+        pack_w(1, 1)
+        direction_term(4, 0)
+        quantize_chan(0, 0)
+        quantize_chan(0, 1)
+        dx_matmul(0, 0)
+        direction_term(4, 1)
+        dx_matmul(1, 0)
+        quantize_w(1)
+
+        round_dz(4)
+        quantize_pos(4)
+        dw_matmul(6)
+        dw_matmul(7)
+        dx_matmul(2, 0)
+        dx_matmul(3, 0)
+        pack_chan(1, 1, nc.scalar.copy)
+        pack_chan(1, 0, nc.vector.tensor_copy)
+        dw_store(6)
+        dw_store(7)
+        quantize_chan(1, 1)
+        quantize_chan(1, 0)
+        for a in range(4):
+            dx_matmul(a, 1)
+            dx_store(a, (nc.vector.tensor_copy, nc.scalar.copy)[a % 2])

@@ -70,9 +70,9 @@ def tile_mdlstmcellweights_pb_v_kernel(
         def load_w(g):
             nc.sync.dma_start(out=w_raw[g][:], in_=slabs_of(w_io, g * PACK, PACK))
 
+        nc.scalar.dma_start(out=ws[:], in_=weighted_sum.partition_broadcast(P))
         load_gate(0, 0)
         load_cell(0, 0)
-        nc.sync.dma_start(out=ws[:], in_=weighted_sum.partition_broadcast(P))
         load_gate(0, 1)
         load_cell(0, 1)
         load_grad(0)
@@ -173,46 +173,41 @@ def tile_mdlstmcellweights_pb_v_kernel(
             quantize(w_codes[g], slice(0, IN_C), w_packed[g][:], E4M3)
 
         def gate_slope(i, d0, d1):
-            width = LOADS[i][1] * HALF
+            width = LOADS[i][1] * N
             if d0 == 0:
-                slope[i] = sb.tile([P, 2, 2 * width], F32, name="slope%d" % i, tag="slope", bufs=2)
-            o = by_half(gates[i][:, d0:d1].rearrange("p d j n -> p (d j n)"))
-            for u in range(2):
-                nc.vector.scalar_tensor_tensor(
-                    out=slope[i][:, u, d0 * width : d1 * width].rearrange("p (k e) -> p k e", e=2),
-                    in0=o[:, u],
-                    scalar=1.0,
-                    in1=o[:, u],
-                    op0=ALU.subtract,
-                    op1=ALU.mult,
-                )
+                slope[i] = sb.tile([P, 2 * width], F32, name="slope%d" % i, tag="slope", bufs=2)
+            o = gates[i][:, d0:d1].rearrange("p d j n -> p (d j n)")
+            nc.vector.scalar_tensor_tensor(
+                out=slope[i][:, d0 * width : d1 * width], in0=o, scalar=1.0, in1=o, op0=ALU.subtract, op1=ALU.mult
+            )
 
         def direction_term(i, d):
             s0, count = LOADS[i]
             width = count * HALF
             q = sb.tile([P, 2, width], F32, name="term%d_%d" % (i, d), tag="term", bufs=2)
-            nc.vector.scalar_tensor_tensor(
-                out=q[:],
-                in0=tanhs[i, d][:],
-                scalar=ws[:, d : d + 1],
-                in1=slope[i][:, :, d * width : (d + 1) * width],
-                op0=ALU.mult,
-                op1=ALU.mult,
-            )
-            for jj in range(count):
-                s = s0 + jj
-                if d == 0:
-                    sums[s] = ps.tile([P, PACK, P], F32, name="sum%d" % s, tag="sum", bufs=3)
-                for t in range(PACK):
-                    u, e = divmod(t, 2)
-                    nc.tensor.matmul(
-                        sums[s][:, t, :],
-                        lhsT=q[:, u, jj * HALF + e : (jj + 1) * HALF : 2],
-                        rhs=ident[:],
-                        is_transpose=True,
-                        start=(d == 0 and t == 0),
-                        stop=(d == 1 and t == PACK - 1),
-                    )
+            for u in range(2):
+                nc.vector.scalar_tensor_tensor(
+                    out=q[:, u, :].rearrange("p (k e) -> p k e", e=2),
+                    in0=tanhs[i, d][:, u, :].rearrange("p (k e) -> p k e", e=2),
+                    scalar=ws[:, d : d + 1],
+                    in1=by_half(slope[i][:, d * 2 * width : (d + 1) * 2 * width])[:, u],
+                    op0=ALU.mult,
+                    op1=ALU.mult,
+                )
+                for jj in range(count):
+                    s = s0 + jj
+                    if d == 0 and u == 0:
+                        sums[s] = ps.tile([P, PACK, P], F32, name="sum%d" % s, tag="sum", bufs=3)
+                    for e in range(2):
+                        t = 2 * u + e
+                        nc.tensor.matmul(
+                            sums[s][:, t, :],
+                            lhsT=q[:, u, jj * HALF + e : (jj + 1) * HALF : 2],
+                            rhs=ident[:],
+                            is_transpose=True,
+                            start=(d == 0 and t == 0),
+                            stop=(d == 1 and t == PACK - 1),
+                        )
 
         def round_dz(i):
             s0, count = LOADS[i]
@@ -361,19 +356,19 @@ def tile_mdlstmcellweights_pb_v_kernel(
         dw_store(4)
         dw_store(5)
         pack_w(1, 1)
-        direction_term(4, 0)
         quantize_chan(0, 0)
         quantize_chan(0, 1)
         dx_matmul(0, 0)
+        direction_term(4, 0)
         direction_term(4, 1)
         dx_matmul(1, 0)
         quantize_w(1)
 
         round_dz(4)
         quantize_pos(4)
+        dx_matmul(2, 0)
         dw_matmul(6)
         dw_matmul(7)
-        dx_matmul(2, 0)
         dx_matmul(3, 0)
         pack_chan(1, 1, nc.scalar.copy)
         pack_chan(1, 0, nc.vector.tensor_copy)

@@ -76,25 +76,29 @@ def tile_mdlstmcellweights_pb_v_kernel(
         load_gate(0, 1)
         load_cell(0, 1)
         load_grad(0)
-        for i in (1, 2):
-            for d in range(2):
-                load_gate(i, d)
-            for d in range(2):
-                load_cell(i, d)
-            load_grad(i)
-        for d in range(2):
-            load_cell(3, d)
+        load_gate(1, 0)
+        load_cell(1, 0)
+        load_gate(1, 1)
+        load_cell(1, 1)
+        load_grad(1)
+        load_gate(2, 0)
+        load_cell(2, 0)
+        load_cell(2, 1)
+        load_grad(2)
+        load_cell(3, 0)
+        load_gate(2, 1)
+        load_cell(3, 1)
         nc.sync.dma_start(out=x_raw[:], in_=x.rearrange("(p a) n -> p a n", a=PACK))
-        for d in range(2):
-            load_gate(3, d)
-        for d in range(2):
-            load_cell(4, d)
+        load_gate(3, 0)
         load_w(0)
         load_grad(3)
-        for d in range(2):
-            load_gate(4, d)
-        load_grad(4)
+        load_cell(4, 0)
+        load_gate(3, 1)
+        load_cell(4, 1)
+        load_gate(4, 0)
         load_w(1)
+        load_grad(4)
+        load_gate(4, 1)
 
         tanhs, grad_t, slope, term, sums, dz_pos, pos_codes = {}, {}, {}, {}, {}, {}, {}
         back, dz_chan, chan_codes, w_packed, w_codes, dw_acc, dx_acc = {}, {}, {}, {}, {}, {}, {}
@@ -115,8 +119,8 @@ def tile_mdlstmcellweights_pb_v_kernel(
             count = LOADS[i][1]
             t = sb.tile([P, 2, count * HALF], F32, name="tanh%d_%d" % (i, d))
             nc.scalar.activation(
-                out=t[:].rearrange("p u (k e) -> p u k e", e=2),
-                in_=by_half(cells[i][d][:].rearrange("p j n -> p (j n)")),
+                out=t[:].rearrange("p u (e k) -> p u e k", e=2),
+                in_=cells[i][d][:].rearrange("p j n -> p (j n)").rearrange("p (k u e) -> p u e k", u=2, e=2),
                 func=ACT.Tanh,
             )
             tanhs[i, d] = t
@@ -168,41 +172,52 @@ def tile_mdlstmcellweights_pb_v_kernel(
                 in_=w_raw[g][:].rearrange("p j (c i) -> p c j i", i=4)[:, cols],
             )
 
-        def quantize_w(g):
-            w_codes[g] = mx_tiles("w%d" % g, IN_C)
-            quantize(w_codes[g], slice(0, IN_C), w_packed[g][:], E4M3)
+        def quantize_w(g, c0=0, c1=IN_C):
+            if c0 == 0:
+                w_codes[g] = mx_tiles("w%d" % g, IN_C)
+            quantize(w_codes[g], slice(c0, c1), w_packed[g][:, c0 * PACK : c1 * PACK], E4M3)
 
         def gate_slope(i, d0, d1):
             width = LOADS[i][1] * N
             if d0 == 0:
                 slope[i] = sb.tile([P, 2 * width], F32, name="slope%d" % i, tag="slope", bufs=2)
-            o = gates[i][:, d0:d1].rearrange("p d j n -> p (d j n)")
-            nc.vector.scalar_tensor_tensor(
-                out=slope[i][:, d0 * width : d1 * width], in0=o, scalar=1.0, in1=o, op0=ALU.subtract, op1=ALU.mult
-            )
-
-        def direction_term(i, d):
-            s0, count = LOADS[i]
-            width = count * HALF
-            q = sb.tile([P, 2, width], F32, name="term%d_%d" % (i, d), tag="term", bufs=2)
+            o = by_half(gates[i][:, d0].rearrange("p j n -> p (j n)"))
             for u in range(2):
                 nc.vector.scalar_tensor_tensor(
-                    out=q[:, u, :].rearrange("p (k e) -> p k e", e=2),
-                    in0=tanhs[i, d][:, u, :].rearrange("p (k e) -> p k e", e=2),
+                    out=slope[i][:, d0 * width : d1 * width].rearrange("p (u k e) -> p u k e", u=2, e=2)[:, u],
+                    in0=o[:, u],
+                    scalar=1.0,
+                    in1=o[:, u],
+                    op0=ALU.subtract,
+                    op1=ALU.mult,
+                )
+
+        def direction_term(i, d, j0=0, per=None):
+            s0, count = LOADS[i]
+            width = count * HALF
+            if j0 == 0:
+                term[i, d] = sb.tile([P, 2, width], F32, name="term%d_%d" % (i, d), tag="term", bufs=2)
+            q = term[i, d]
+            per = per or count
+            for u in range(2):
+                words = slice(j0 * P, (j0 + per) * P)
+                nc.vector.scalar_tensor_tensor(
+                    out=q[:, u, :].rearrange("p (e k) -> p e k", e=2)[:, :, words],
+                    in0=tanhs[i, d][:, u, :].rearrange("p (e k) -> p e k", e=2)[:, :, words],
                     scalar=ws[:, d : d + 1],
-                    in1=by_half(slope[i][:, d * 2 * width : (d + 1) * 2 * width])[:, u],
+                    in1=slope[i][:, d * 2 * width : (d + 1) * 2 * width].rearrange("p (u k e) -> p u e k", u=2, e=2)[:, u, :, words],
                     op0=ALU.mult,
                     op1=ALU.mult,
                 )
-                for jj in range(count):
+                for jj in range(j0, j0 + per):
                     s = s0 + jj
                     if d == 0 and u == 0:
-                        sums[s] = ps.tile([P, PACK, P], F32, name="sum%d" % s, tag="sum", bufs=3)
+                        sums[s] = ps.tile([P, PACK, P], F32, name="sum%d" % s, tag="sum%d" % (s % 3))
                     for e in range(2):
                         t = 2 * u + e
                         nc.tensor.matmul(
                             sums[s][:, t, :],
-                            lhsT=q[:, u, jj * HALF + e : (jj + 1) * HALF : 2],
+                            lhsT=q[:, u, (e * count + jj) * P : (e * count + jj + 1) * P],
                             rhs=ident[:],
                             is_transpose=True,
                             start=(d == 0 and t == 0),
@@ -267,8 +282,8 @@ def tile_mdlstmcellweights_pb_v_kernel(
 
         def dx_matmul(a, g):
             if g == 0:
-                tag, bufs = (("grad", 1), ("sum", 3), ("sum", 3), ("sum", 3))[a]
-                dx_acc[a] = ps.tile([P, N], F32, name="dx_acc%d" % a, tag=tag, bufs=bufs)
+                tag = ("sum2", "grad", "sum0", "sum1")[a]
+                dx_acc[a] = ps.tile([P, N], F32, name="dx_acc%d" % a, tag=tag)
             cols = slice(a * P, (a + 1) * P)
             nc.tensor.matmul_mx(
                 out=dx_acc[a][:],
@@ -291,17 +306,18 @@ def tile_mdlstmcellweights_pb_v_kernel(
         tanh_of(0, 0)
         gate_slope(0, 0, 1)
         tanh_of(0, 1)
-        direction_term(0, 0)
         gate_slope(0, 1, 2)
         turn_grad(0)
         pack_grad(0)
+        direction_term(0, 0)
         direction_term(0, 1)
         tanh_of(1, 0)
         tanh_of(1, 1)
 
         turn_grad(1)
         pack_grad(1)
-        gate_slope(1, 0, 2)
+        gate_slope(1, 0, 1)
+        gate_slope(1, 1, 2)
         round_dz(0)
         direction_term(1, 0)
         quantize_pos(0)
@@ -311,71 +327,82 @@ def tile_mdlstmcellweights_pb_v_kernel(
 
         turn_grad(2)
         pack_grad(2)
-        gate_slope(2, 0, 2)
-        round_dz(1)
         tanh_of(3, 0)
         tanh_of(3, 1)
+        gate_slope(2, 0, 1)
+        round_dz(1)
+        direction_term(2, 0)
         turn_x()
         pack_x()
-        direction_term(2, 0)
+        gate_slope(2, 1, 2)
         quantize_pos(1)
         direction_term(2, 1)
-        tanh_of(4, 0)
-        tanh_of(4, 1)
+        pack_w(0, 0)
+        pack_w(0, 1)
 
-        gate_slope(3, 0, 2)
-        quantize(x_codes, slice(0, IN_C), x_packed[:], E4M3)
         turn_grad(3)
+        pack_grad(3)
+        gate_slope(3, 0, 1)
+        quantize(x_codes, slice(0, IN_C), x_packed[:], E4M3)
         dw_matmul(0)
         dw_matmul(1)
         round_dz(2)
-        pack_w(0, 0)
+        tanh_of(4, 0)
         dw_store(0)
         dw_store(1)
-        pack_grad(3)
         pack_chan(0, 0, nc.scalar.copy)
         pack_chan(0, 1, nc.scalar.copy)
         direction_term(3, 0)
         quantize_pos(2)
         dw_matmul(2)
         dw_matmul(3)
+        gate_slope(3, 1, 2)
+        quantize_w(0)
         direction_term(3, 1)
-        pack_w(0, 1)
         dw_store(2)
         dw_store(3)
+        tanh_of(4, 1)
 
         turn_grad(4)
         pack_grad(4)
-        gate_slope(4, 0, 2)
+        gate_slope(4, 0, 1)
         round_dz(3)
-        pack_w(1, 0)
-        quantize_w(0)
+        quantize_chan(0, 0)
         quantize_pos(3)
         dw_matmul(4)
         dw_matmul(5)
+        quantize_chan(0, 1)
+        dx_matmul(0, 0)
+        pack_w(1, 0)
         dw_store(4)
         dw_store(5)
         pack_w(1, 1)
-        quantize_chan(0, 0)
-        quantize_chan(0, 1)
-        dx_matmul(0, 0)
-        direction_term(4, 0)
-        direction_term(4, 1)
+        gate_slope(4, 1, 2)
+        direction_term(4, 0, 0, 1)
+        direction_term(4, 1, 0, 1)
+        direction_term(4, 0, 1, 1)
+        direction_term(4, 1, 1, 1)
         dx_matmul(1, 0)
-        quantize_w(1)
 
         round_dz(4)
         quantize_pos(4)
-        dx_matmul(2, 0)
         dw_matmul(6)
         dw_matmul(7)
+        dx_matmul(2, 0)
         dx_matmul(3, 0)
         pack_chan(1, 1, nc.scalar.copy)
         pack_chan(1, 0, nc.vector.tensor_copy)
+        quantize_w(1, 0, HALF)
         dw_store(6)
         dw_store(7)
         quantize_chan(1, 1)
         quantize_chan(1, 0)
-        for a in range(4):
-            dx_matmul(a, 1)
-            dx_store(a, (nc.vector.tensor_copy, nc.scalar.copy)[a % 2])
+        quantize_w(1, HALF, IN_C)
+        dx_matmul(0, 1)
+        dx_store(0, nc.vector.tensor_copy)
+        dx_matmul(1, 1)
+        dx_store(1, nc.scalar.copy)
+        dx_matmul(2, 1)
+        dx_store(2, nc.vector.tensor_copy)
+        dx_matmul(3, 1)
+        dx_store(3, nc.scalar.copy)

@@ -119,8 +119,8 @@ def tile_mdlstmcellweights_pb_v_kernel(
             count = LOADS[i][1]
             t = sb.tile([P, 2, count * HALF], F32, name="tanh%d_%d" % (i, d))
             nc.scalar.activation(
-                out=t[:].rearrange("p u (e k) -> p u e k", e=2),
-                in_=cells[i][d][:].rearrange("p j n -> p (j n)").rearrange("p (k u e) -> p u e k", u=2, e=2),
+                out=t[:].rearrange("p u (k e) -> p u k e", e=2),
+                in_=by_half(cells[i][d][:].rearrange("p j n -> p (j n)")),
                 func=ACT.Tanh,
             )
             tanhs[i, d] = t
@@ -181,16 +181,10 @@ def tile_mdlstmcellweights_pb_v_kernel(
             width = LOADS[i][1] * N
             if d0 == 0:
                 slope[i] = sb.tile([P, 2 * width], F32, name="slope%d" % i, tag="slope", bufs=2)
-            o = by_half(gates[i][:, d0].rearrange("p j n -> p (j n)"))
-            for u in range(2):
-                nc.vector.scalar_tensor_tensor(
-                    out=slope[i][:, d0 * width : d1 * width].rearrange("p (u k e) -> p u k e", u=2, e=2)[:, u],
-                    in0=o[:, u],
-                    scalar=1.0,
-                    in1=o[:, u],
-                    op0=ALU.subtract,
-                    op1=ALU.mult,
-                )
+            o = gates[i][:, d0:d1].rearrange("p d j n -> p (d j n)")
+            nc.vector.scalar_tensor_tensor(
+                out=slope[i][:, d0 * width : d1 * width], in0=o, scalar=1.0, in1=o, op0=ALU.subtract, op1=ALU.mult
+            )
 
         def direction_term(i, d, j0=0, per=None):
             s0, count = LOADS[i]
@@ -202,10 +196,10 @@ def tile_mdlstmcellweights_pb_v_kernel(
             for u in range(2):
                 words = slice(j0 * P, (j0 + per) * P)
                 nc.vector.scalar_tensor_tensor(
-                    out=q[:, u, :].rearrange("p (e k) -> p e k", e=2)[:, :, words],
-                    in0=tanhs[i, d][:, u, :].rearrange("p (e k) -> p e k", e=2)[:, :, words],
+                    out=q[:, u, :].rearrange("p (k e) -> p k e", e=2)[:, words],
+                    in0=tanhs[i, d][:, u, :].rearrange("p (k e) -> p k e", e=2)[:, words],
                     scalar=ws[:, d : d + 1],
-                    in1=slope[i][:, d * 2 * width : (d + 1) * 2 * width].rearrange("p (u k e) -> p u e k", u=2, e=2)[:, u, :, words],
+                    in1=by_half(slope[i][:, d * 2 * width : (d + 1) * 2 * width])[:, u, words],
                     op0=ALU.mult,
                     op1=ALU.mult,
                 )
@@ -217,7 +211,7 @@ def tile_mdlstmcellweights_pb_v_kernel(
                         t = 2 * u + e
                         nc.tensor.matmul(
                             sums[s][:, t, :],
-                            lhsT=q[:, u, (e * count + jj) * P : (e * count + jj + 1) * P],
+                            lhsT=q[:, u, jj * HALF + e : (jj + 1) * HALF : 2],
                             rhs=ident[:],
                             is_transpose=True,
                             start=(d == 0 and t == 0),
@@ -367,24 +361,23 @@ def tile_mdlstmcellweights_pb_v_kernel(
         pack_grad(4)
         gate_slope(4, 0, 1)
         round_dz(3)
-        quantize_chan(0, 0)
+        direction_term(4, 0)
         quantize_pos(3)
         dw_matmul(4)
         dw_matmul(5)
-        quantize_chan(0, 1)
-        dx_matmul(0, 0)
         pack_w(1, 0)
         dw_store(4)
         dw_store(5)
         pack_w(1, 1)
         gate_slope(4, 1, 2)
-        direction_term(4, 0, 0, 1)
+        quantize_chan(0, 0)
         direction_term(4, 1, 0, 1)
-        direction_term(4, 0, 1, 1)
         direction_term(4, 1, 1, 1)
-        dx_matmul(1, 0)
+        quantize_chan(0, 1)
+        dx_matmul(0, 0)
 
         round_dz(4)
+        dx_matmul(1, 0)
         quantize_pos(4)
         dw_matmul(6)
         dw_matmul(7)

@@ -19,9 +19,9 @@ ACT = mybir.ActivationFunctionType
 P = 128
 PACK = 4
 PASSES = OUT_C // (P * PACK)
-SLABS = PASSES * PACK
 HALF = N // 2
-LOADS = [(0, 1), (1, 1), (2, 2), (4, 2), (6, 2)]
+SUM_BANKS = 3
+CHUNKS = [(0, 1), (1, 1), (2, 2), (4, 2), (6, 2)]
 
 
 def tile_mdlstmcellweights_pb_v_kernel(
@@ -29,17 +29,14 @@ def tile_mdlstmcellweights_pb_v_kernel(
 ):
     nc = tc.nc
 
-    def slabs_of(t, s0, count):
-        g, j = divmod(s0, PACK)
-        return t.rearrange("(g p j) n -> p g j n", p=P, j=PACK)[:, g, j : j + count, :]
+    def slabs_of(hbm, first, count):
+        g, j = divmod(first, PACK)
+        return hbm.rearrange("(g p j) n -> p g j n", p=P, j=PACK)[:, g, j : j + count, :]
 
-    def by_half(ap):
+    def by_pair(ap):
         return ap.rearrange("p (k u e) -> p u k e", u=2, e=2)
 
-    load_of = {}
-    for i, (s0, count) in enumerate(LOADS):
-        for jj in range(count):
-            load_of[s0 + jj] = (i, jj)
+    chunk_of = {first + jj: (i, jj) for i, (first, count) in enumerate(CHUNKS) for jj in range(count)}
 
     with ExitStack() as ctx:
         sb = ctx.enter_context(tc.tile_pool(name="sb", bufs=1))
@@ -50,7 +47,7 @@ def tile_mdlstmcellweights_pb_v_kernel(
         make_identity(nc, ident[:])
 
         gates, cells, grads = [], [], []
-        for i, (s0, count) in enumerate(LOADS):
+        for i, (first, count) in enumerate(CHUNKS):
             gates.append(sb.tile([P, 2, count, N], F32, name="gates%d" % i))
             cells.append([sb.tile([P, count, N], BF16, name="cell%d_%d" % (i, d)) for d in range(2)])
             grads.append(sb.tile([P, count, N], BF16, name="grad%d" % i))
@@ -59,28 +56,23 @@ def tile_mdlstmcellweights_pb_v_kernel(
         w_raw = [sb.tile([P, PACK, IN_C], BF16, name="w_raw%d" % g) for g in range(PASSES)]
 
         def load_gate(i, d):
-            nc.sync.dma_start(out=gates[i][:, d], in_=slabs_of((o_dim0, o_dim1)[d], *LOADS[i]))
+            nc.sync.dma_start(out=gates[i][:, d], in_=slabs_of((o_dim0, o_dim1)[d], *CHUNKS[i]))
 
         def load_cell(i, d):
-            nc.sync.dma_start(out=cells[i][d][:], in_=slabs_of((ct0, ct1)[d], *LOADS[i]))
+            nc.sync.dma_start(out=cells[i][d][:], in_=slabs_of((ct0, ct1)[d], *CHUNKS[i]))
 
         def load_grad(i):
-            nc.sync.dma_start(out=grads[i][:], in_=slabs_of(grad_out, *LOADS[i]))
+            nc.sync.dma_start(out=grads[i][:], in_=slabs_of(grad_out, *CHUNKS[i]))
 
         def load_w(g):
             nc.sync.dma_start(out=w_raw[g][:], in_=slabs_of(w_io, g * PACK, PACK))
 
         nc.scalar.dma_start(out=ws[:], in_=weighted_sum.partition_broadcast(P))
-        load_gate(0, 0)
-        load_cell(0, 0)
-        load_gate(0, 1)
-        load_cell(0, 1)
-        load_grad(0)
-        load_gate(1, 0)
-        load_cell(1, 0)
-        load_gate(1, 1)
-        load_cell(1, 1)
-        load_grad(1)
+        for i in range(2):
+            for d in range(2):
+                load_gate(i, d)
+                load_cell(i, d)
+            load_grad(i)
         load_gate(2, 0)
         load_cell(2, 0)
         load_cell(2, 1)
@@ -100,9 +92,10 @@ def tile_mdlstmcellweights_pb_v_kernel(
         load_grad(4)
         load_gate(4, 1)
 
-        tanhs, grad_t, slope, term, sums, dz_pos, pos_codes = {}, {}, {}, {}, {}, {}, {}
-        back, dz_chan, chan_codes, w_packed, w_codes, dw_acc, dx_acc = {}, {}, {}, {}, {}, {}, {}
-        grad_bank, x_bank = {}, {}
+        tanhs, slopes, terms, sums = {}, {}, {}, {}
+        grad_bank, grad_pos, dz_pos, pos_mx = {}, {}, {}, {}
+        back, dz_chan, chan_mx = {}, {}, {}
+        x_bank, w_packed, w_mx, dw_acc, dx_acc = {}, {}, {}, {}, {}
         x_packed = sb.tile([P, IN_C * PACK], BF16, name="x_packed", align_bytes=64)
 
         def mx_tiles(name, width):
@@ -110,108 +103,117 @@ def tile_mdlstmcellweights_pb_v_kernel(
             scales = sb.tile([P, width], U8, name=name + "_scales", align_bytes=64)
             return codes, scales
 
-        x_codes = mx_tiles("x", IN_C)
+        x_mx = mx_tiles("x", IN_C)
 
-        def quantize(dst, cols, src, fmt):
-            nc.vector.quantize_mx(out=dst[0][:, cols].bitcast(fmt), scales=dst[1][:, cols], in_=src)
+        ws_neg = sb.tile([P, 2], F32, name="ws_neg")
+        nc.vector.tensor_scalar_mul(ws_neg[:], ws[:], -1.0)
 
-        def tanh_of(i, d):
-            count = LOADS[i][1]
-            t = sb.tile([P, 2, count * HALF], F32, name="tanh%d_%d" % (i, d))
-            nc.scalar.activation(
-                out=t[:].rearrange("p u (k e) -> p u k e", e=2),
-                in_=by_half(cells[i][d][:].rearrange("p j n -> p (j n)")),
-                func=ACT.Tanh,
+        def quantize(mx, cols, src, fmt):
+            nc.vector.quantize_mx(out=mx[0][:, cols].bitcast(fmt), scales=mx[1][:, cols], in_=src)
+
+        def matmul_mx(acc, lhs, cols, lhs_fmt, rhs, rhs_fmt, start, stop):
+            nc.tensor.matmul_mx(
+                out=acc[:],
+                lhsT=lhs[0][:, cols].bitcast(lhs_fmt),
+                lhsT_scale=lhs[1][:, cols],
+                rhs=rhs[0][:].bitcast(rhs_fmt),
+                rhs_scale=rhs[1][:],
+                start=start,
+                stop=stop,
             )
-            tanhs[i, d] = t
 
-        def turn_grad(i):
-            count = LOADS[i][1]
-            words = grads[i][:].rearrange("p j n -> p (j n)").bitcast(F32)
-            bank = ps.tile([P, count * 2, P], F32, name="grad_bank%d" % i, tag="grad")
-            for jj in range(count):
-                for u in range(2):
-                    nc.tensor.transpose(bank[:, 2 * jj + u, :], words[:, jj * HALF + u : (jj + 1) * HALF : 2], ident[:])
-            grad_bank[i] = bank
+        def turn_pairs(bank, pairs, row, u):
+            nc.tensor.transpose(bank, pairs[:, row * HALF + u : (row + 1) * HALF : 2], ident[:])
 
-        def pack_grad(i):
-            count = LOADS[i][1]
-            bank = grad_bank[i]
-            gt = sb.tile([P, count * N], BF16, name="grad_t%d" % i)
-            nc.scalar.copy(
-                out=gt[:].bitcast(F32).rearrange("p (j c u) -> p j c u", j=count, u=2),
-                in_=bank[:].rearrange("p (j u) c -> p j c u", u=2),
-            )
-            grad_t[i] = gt
 
         def turn_x():
-            words = x_raw[:].rearrange("p a n -> p (a n)").bitcast(F32)
+            pairs = x_raw[:].rearrange("p a n -> p (a n)").bitcast(F32)
             for h in range(2):
-                bank = ps.tile([P, 4, P], F32, name="x_bank%d" % h, tag="dw", bufs=2)
-                for a in range(2 * h, 2 * h + 2):
+                x_bank[h] = ps.tile([P, 4, P], F32, name="x_bank%d" % h, tag="dw", bufs=2)
+                for a in range(2):
                     for u in range(2):
-                        nc.tensor.transpose(
-                            bank[:, 2 * (a % 2) + u, :], words[:, a * HALF + u : (a + 1) * HALF : 2], ident[:]
-                        )
-                x_bank[h] = bank
+                        turn_pairs(x_bank[h][:, 2 * a + u, :], pairs, 2 * h + a, u)
 
         def pack_x():
             for h in range(2):
-                bank = x_bank[h]
                 nc.scalar.copy(
-                    out=x_packed[:].bitcast(F32).rearrange("q (p h k) -> q h p k", h=2, k=4)[:, h],
-                    in_=bank[:].rearrange("q k p -> q p k"),
+                    out=x_packed[:].bitcast(F32).rearrange("m (p h k) -> m h p k", h=2, k=4)[:, h],
+                    in_=x_bank[h][:].rearrange("m k p -> m p k"),
                 )
 
-        def pack_w(g, half, copy=nc.scalar.copy):
+        def pack_w(g, half):
             if half == 0:
                 w_packed[g] = sb.tile([P, IN_C * PACK], BF16, name="w_packed%d" % g, align_bytes=64)
-            cols = slice(half * 64, half * 64 + 64)
-            copy(
-                out=w_packed[g][:].rearrange("p (c i j) -> p c j i", i=4, j=PACK)[:, cols],
-                in_=w_raw[g][:].rearrange("p j (c i) -> p c j i", i=4)[:, cols],
+            fours = slice(half * HALF // 4, (half + 1) * HALF // 4)
+            nc.scalar.copy(
+                out=w_packed[g][:].rearrange("p (k i j) -> p k j i", i=4, j=PACK)[:, fours],
+                in_=w_raw[g][:].rearrange("p j (k i) -> p k j i", i=4)[:, fours],
             )
 
-        def quantize_w(g, c0=0, c1=IN_C):
+        def quantize_w(g, c0, c1):
             if c0 == 0:
-                w_codes[g] = mx_tiles("w%d" % g, IN_C)
-            quantize(w_codes[g], slice(c0, c1), w_packed[g][:, c0 * PACK : c1 * PACK], E4M3)
+                w_mx[g] = mx_tiles("w%d" % g, IN_C)
+            quantize(w_mx[g], slice(c0, c1), w_packed[g][:, c0 * PACK : c1 * PACK], E4M3)
 
-        def gate_slope(i, d0, d1):
-            width = LOADS[i][1] * N
-            if d0 == 0:
-                slope[i] = sb.tile([P, 2 * width], F32, name="slope%d" % i, tag="slope", bufs=2)
-            o = gates[i][:, d0:d1].rearrange("p d j n -> p (d j n)")
-            nc.vector.scalar_tensor_tensor(
-                out=slope[i][:, d0 * width : d1 * width], in0=o, scalar=1.0, in1=o, op0=ALU.subtract, op1=ALU.mult
+
+        def tanh_of(i, d):
+            count = CHUNKS[i][1]
+            tanhs[i, d] = sb.tile([P, 2, count * HALF], F32, name="tanh%d_%d" % (i, d))
+            nc.scalar.activation(
+                out=tanhs[i, d][:].rearrange("p u (k e) -> p u k e", e=2),
+                in_=by_pair(cells[i][d][:].rearrange("p j n -> p (j n)")),
+                func=ACT.Tanh,
             )
 
-        def direction_term(i, d, j0=0, per=None):
-            s0, count = LOADS[i]
-            width = count * HALF
-            if j0 == 0:
-                term[i, d] = sb.tile([P, 2, width], F32, name="term%d_%d" % (i, d), tag="term", bufs=2)
-            q = term[i, d]
-            per = per or count
+        def turn_grad(i):
+            count = CHUNKS[i][1]
+            pairs = grads[i][:].rearrange("p j n -> p (j n)").bitcast(F32)
+            grad_bank[i] = ps.tile([P, count * 2, P], F32, name="grad_bank%d" % i, tag="grad")
+            for jj in range(count):
+                for u in range(2):
+                    turn_pairs(grad_bank[i][:, 2 * jj + u, :], pairs, jj, u)
+
+        def pack_grad(i):
+            count = CHUNKS[i][1]
+            grad_pos[i] = sb.tile([P, count * N], BF16, name="grad_t%d" % i)
+            nc.scalar.copy(
+                out=grad_pos[i][:].bitcast(F32).rearrange("m (j p u) -> m j p u", j=count, u=2),
+                in_=grad_bank[i][:].rearrange("m (j u) p -> m j p u", u=2),
+            )
+
+        def gate_slope(i, d):
+            width = CHUNKS[i][1] * N
+            if d == 0:
+                slopes[i] = sb.tile([P, 2 * width], F32, name="slope%d" % i, tag="slope", bufs=2)
+            o = gates[i][:, d : d + 1].rearrange("p d j n -> p (d j n)")
+            nc.vector.scalar_tensor_tensor(
+                out=slopes[i][:, d * width : (d + 1) * width], in0=o, scalar=1.0, in1=o, op0=ALU.subtract, op1=ALU.mult
+            )
+
+        def direction_term(i, d, jj0, jj1):
+            first, count = CHUNKS[i]
+            if jj0 == 0:
+                terms[i, d] = sb.tile([P, 2, count * HALF], F32, name="term%d_%d" % (i, d), tag="term", bufs=2)
+            term = terms[i, d]
+            ks = slice(jj0 * P, jj1 * P)
             for u in range(2):
-                words = slice(j0 * P, (j0 + per) * P)
                 nc.vector.scalar_tensor_tensor(
-                    out=q[:, u, :].rearrange("p (k e) -> p k e", e=2)[:, words],
-                    in0=tanhs[i, d][:, u, :].rearrange("p (k e) -> p k e", e=2)[:, words],
-                    scalar=ws[:, d : d + 1],
-                    in1=by_half(slope[i][:, d * 2 * width : (d + 1) * 2 * width])[:, u, words],
+                    out=term[:, u, :].rearrange("p (k e) -> p k e", e=2)[:, ks],
+                    in0=tanhs[i, d][:, u, :].rearrange("p (k e) -> p k e", e=2)[:, ks],
+                    scalar=ws_neg[:, d : d + 1],
+                    in1=by_pair(slopes[i][:, d * count * N : (d + 1) * count * N])[:, u, ks],
                     op0=ALU.mult,
                     op1=ALU.mult,
                 )
-                for jj in range(j0, j0 + per):
-                    s = s0 + jj
+                for jj in range(jj0, jj1):
+                    s = first + jj
                     if d == 0 and u == 0:
-                        sums[s] = ps.tile([P, PACK, P], F32, name="sum%d" % s, tag="sum%d" % (s % 3))
+                        sums[s] = ps.tile([P, PACK, P], F32, name="sum%d" % s, tag="sum%d" % (s % SUM_BANKS))
                     for e in range(2):
                         t = 2 * u + e
                         nc.tensor.matmul(
                             sums[s][:, t, :],
-                            lhsT=q[:, u, jj * HALF + e : (jj + 1) * HALF : 2],
+                            lhsT=term[:, u, jj * HALF + e : (jj + 1) * HALF : 2],
                             rhs=ident[:],
                             is_transpose=True,
                             start=(d == 0 and t == 0),
@@ -219,29 +221,27 @@ def tile_mdlstmcellweights_pb_v_kernel(
                         )
 
         def round_dz(i):
-            s0, count = LOADS[i]
+            first, count = CHUNKS[i]
             dz_pos[i] = sb.tile([P, count * N], BF16, name="dz_pos%d" % i, align_bytes=64)
-            words = dz_pos[i][:].bitcast(F32)
+            pairs = dz_pos[i][:].bitcast(F32)
             for jj in range(count):
                 cols = slice(jj * N, (jj + 1) * N)
-                nc.vector.scalar_tensor_tensor(
-                    out=dz_pos[i][:, cols].rearrange("p (c t) -> p c t", t=PACK),
-                    in0=sums[s0 + jj][:].rearrange("p t c -> p c t"),
-                    scalar=-1.0,
-                    in1=grad_t[i][:, cols].rearrange("p (c t) -> p c t", t=PACK),
-                    op0=ALU.mult,
-                    op1=ALU.mult,
+                nc.vector.tensor_tensor(
+                    out=dz_pos[i][:, cols].rearrange("m (k r t) -> m k t r", r=2, t=PACK),
+                    in0=sums[first + jj][:].rearrange("m t (k r) -> m k t r", r=2),
+                    in1=grad_pos[i][:, cols].rearrange("m (k r t) -> m k t r", r=2, t=PACK),
+                    op=ALU.mult,
                 )
-                g, j = divmod(s0 + jj, PACK)
+                g, j = divmod(first + jj, PACK)
                 for u in range(2):
                     if j == 0:
                         back[g, u] = ps.tile([P, PACK, P], F32, name="back%d_%d" % (g, u), tag="back%d" % u)
-                    nc.tensor.transpose(back[g, u][:, j, :], words[:, jj * HALF + u : (jj + 1) * HALF : 2], ident[:])
+                    turn_pairs(back[g, u][:, j, :], pairs, jj, u)
 
         def quantize_pos(i):
-            width = LOADS[i][1] * P
-            pos_codes[i] = mx_tiles("pos%d" % i, width)
-            quantize(pos_codes[i], slice(0, width), dz_pos[i][:], E5M2)
+            width = CHUNKS[i][1] * P
+            pos_mx[i] = mx_tiles("pos%d" % i, width)
+            quantize(pos_mx[i], slice(0, width), dz_pos[i][:], E5M2)
 
         def pack_chan(g, u, copy):
             dz_chan[g, u] = sb.tile([P, HALF * PACK], BF16, name="dz_chan%d_%d" % (g, u), align_bytes=64)
@@ -251,43 +251,27 @@ def tile_mdlstmcellweights_pb_v_kernel(
             )
 
         def quantize_chan(g, u):
-            if g not in chan_codes:
-                chan_codes[g] = mx_tiles("chan%d" % g, N)
-            quantize(chan_codes[g], slice(u * HALF, (u + 1) * HALF), dz_chan[g, u][:], E5M2)
+            if g not in chan_mx:
+                chan_mx[g] = mx_tiles("chan%d" % g, N)
+            quantize(chan_mx[g], slice(u * HALF, (u + 1) * HALF), dz_chan[g, u][:], E5M2)
 
-        def dw_matmul(s, tag="dw", bufs=2):
-            i, jj = load_of[s]
-            cols = slice(jj * P, (jj + 1) * P)
-            dw_acc[s] = ps.tile([P, IN_C], F32, name="dw_acc%d" % s, tag=tag, bufs=bufs)
-            nc.tensor.matmul_mx(
-                out=dw_acc[s][:],
-                lhsT=pos_codes[i][0][:, cols].bitcast(E5M2),
-                lhsT_scale=pos_codes[i][1][:, cols],
-                rhs=x_codes[0][:].bitcast(E4M3),
-                rhs_scale=x_codes[1][:],
-                start=True,
-                stop=True,
-            )
 
-        def dw_store(s, copy=nc.scalar.copy):
+        def dw_matmul(s):
+            i, jj = chunk_of[s]
+            dw_acc[s] = ps.tile([P, IN_C], F32, name="dw_acc%d" % s, tag="dw", bufs=2)
+            matmul_mx(dw_acc[s], pos_mx[i], slice(jj * P, (jj + 1) * P), E5M2, x_mx, E4M3, True, True)
+
+        def dw_store(s):
             res = sb.tile([P, 1, IN_C], F32, name="dw%d" % s)
-            copy(out=res[:, 0, :], in_=dw_acc[s][:])
+            nc.scalar.copy(out=res[:, 0, :], in_=dw_acc[s][:])
             nc.sync.dma_start(out=slabs_of(out_1, s, 1), in_=res[:])
+
+        dx_banks = ["sum%d" % (5 % SUM_BANKS), "grad", "sum%d" % (6 % SUM_BANKS), "sum%d" % (7 % SUM_BANKS)]
 
         def dx_matmul(a, g):
             if g == 0:
-                tag = ("sum2", "grad", "sum0", "sum1")[a]
-                dx_acc[a] = ps.tile([P, N], F32, name="dx_acc%d" % a, tag=tag)
-            cols = slice(a * P, (a + 1) * P)
-            nc.tensor.matmul_mx(
-                out=dx_acc[a][:],
-                lhsT=w_codes[g][0][:, cols].bitcast(E4M3),
-                lhsT_scale=w_codes[g][1][:, cols],
-                rhs=chan_codes[g][0][:].bitcast(E5M2),
-                rhs_scale=chan_codes[g][1][:],
-                start=(g == 0),
-                stop=(g == PASSES - 1),
-            )
+                dx_acc[a] = ps.tile([P, N], F32, name="dx_acc%d" % a, tag=dx_banks[a])
+            matmul_mx(dx_acc[a], w_mx[g], slice(a * P, (a + 1) * P), E4M3, chan_mx[g], E5M2, g == 0, g == PASSES - 1)
 
         def dx_store(a, copy):
             res = sb.tile([P, N], F32, name="dx%d" % a)
@@ -297,105 +281,100 @@ def tile_mdlstmcellweights_pb_v_kernel(
             )
             nc.sync.dma_start(out=out_0[a * P : (a + 1) * P, :], in_=res[:])
 
-        tanh_of(0, 0)
-        gate_slope(0, 0, 1)
-        tanh_of(0, 1)
-        gate_slope(0, 1, 2)
+
+        for d in range(2):
+            tanh_of(0, d)
+            gate_slope(0, d)
         turn_grad(0)
         pack_grad(0)
-        direction_term(0, 0)
-        direction_term(0, 1)
-        tanh_of(1, 0)
-        tanh_of(1, 1)
+        for d in range(2):
+            direction_term(0, d, 0, 1)
+        for d in range(2):
+            tanh_of(1, d)
 
         turn_grad(1)
         pack_grad(1)
-        gate_slope(1, 0, 1)
-        gate_slope(1, 1, 2)
+        for d in range(2):
+            gate_slope(1, d)
         round_dz(0)
-        direction_term(1, 0)
+        direction_term(1, 0, 0, 1)
         quantize_pos(0)
-        direction_term(1, 1)
-        tanh_of(2, 0)
-        tanh_of(2, 1)
+        direction_term(1, 1, 0, 1)
+        for d in range(2):
+            tanh_of(2, d)
 
         turn_grad(2)
         pack_grad(2)
-        tanh_of(3, 0)
-        tanh_of(3, 1)
-        gate_slope(2, 0, 1)
+        for d in range(2):
+            tanh_of(3, d)
+        gate_slope(2, 0)
         round_dz(1)
-        direction_term(2, 0)
+        direction_term(2, 0, 0, 2)
         turn_x()
         pack_x()
-        gate_slope(2, 1, 2)
+        gate_slope(2, 1)
         quantize_pos(1)
-        direction_term(2, 1)
-        pack_w(0, 0)
-        pack_w(0, 1)
+        direction_term(2, 1, 0, 2)
+        for half in range(2):
+            pack_w(0, half)
 
         turn_grad(3)
         pack_grad(3)
-        gate_slope(3, 0, 1)
-        quantize(x_codes, slice(0, IN_C), x_packed[:], E4M3)
-        dw_matmul(0)
-        dw_matmul(1)
+        gate_slope(3, 0)
+        quantize(x_mx, slice(0, IN_C), x_packed[:], E4M3)
+        for s in (0, 1):
+            dw_matmul(s)
         round_dz(2)
         tanh_of(4, 0)
-        dw_store(0)
-        dw_store(1)
-        pack_chan(0, 0, nc.scalar.copy)
-        pack_chan(0, 1, nc.scalar.copy)
-        direction_term(3, 0)
+        for s in (0, 1):
+            dw_store(s)
+        for u in range(2):
+            pack_chan(0, u, nc.scalar.copy)
+        direction_term(3, 0, 0, 2)
         quantize_pos(2)
-        dw_matmul(2)
-        dw_matmul(3)
-        gate_slope(3, 1, 2)
-        quantize_w(0)
-        direction_term(3, 1)
-        dw_store(2)
-        dw_store(3)
+        for s in (2, 3):
+            dw_matmul(s)
+        gate_slope(3, 1)
+        quantize_w(0, 0, IN_C)
+        direction_term(3, 1, 0, 2)
+        for s in (2, 3):
+            dw_store(s)
         tanh_of(4, 1)
 
         turn_grad(4)
         pack_grad(4)
-        gate_slope(4, 0, 1)
+        gate_slope(4, 0)
         round_dz(3)
-        direction_term(4, 0)
+        direction_term(4, 0, 0, 2)
         quantize_pos(3)
-        dw_matmul(4)
-        dw_matmul(5)
+        for s in (4, 5):
+            dw_matmul(s)
         pack_w(1, 0)
-        dw_store(4)
-        dw_store(5)
+        for s in (4, 5):
+            dw_store(s)
         pack_w(1, 1)
-        gate_slope(4, 1, 2)
+        gate_slope(4, 1)
         quantize_chan(0, 0)
-        direction_term(4, 1, 0, 1)
-        direction_term(4, 1, 1, 1)
+        for jj in range(2):
+            direction_term(4, 1, jj, jj + 1)
         quantize_chan(0, 1)
         dx_matmul(0, 0)
 
         round_dz(4)
         dx_matmul(1, 0)
         quantize_pos(4)
-        dw_matmul(6)
-        dw_matmul(7)
-        dx_matmul(2, 0)
-        dx_matmul(3, 0)
+        for s in (6, 7):
+            dw_matmul(s)
+        for a in (2, 3):
+            dx_matmul(a, 0)
         pack_chan(1, 1, nc.scalar.copy)
         pack_chan(1, 0, nc.vector.tensor_copy)
         quantize_w(1, 0, HALF)
-        dw_store(6)
-        dw_store(7)
+        for s in (6, 7):
+            dw_store(s)
         quantize_chan(1, 1)
         quantize_chan(1, 0)
         quantize_w(1, HALF, IN_C)
-        dx_matmul(0, 1)
-        dx_store(0, nc.vector.tensor_copy)
-        dx_matmul(1, 1)
-        dx_store(1, nc.scalar.copy)
-        dx_matmul(2, 1)
-        dx_store(2, nc.vector.tensor_copy)
-        dx_matmul(3, 1)
-        dx_store(3, nc.scalar.copy)
+        for a in range(IN_C // P):
+            dx_matmul(a, 1)
+            dx_store(a, (nc.vector.tensor_copy, nc.scalar.copy)[a % 2])

from contextlib import ExitStack

import concourse.mybir as mybir
from concourse.masks import make_identity

IN_C, OUT_C, N = 512, 1024, 512
FLOPS = 2 * 2 * IN_C * OUT_C * N
BYTES = 2 * (IN_C * N + 3 * OUT_C * N + OUT_C * IN_C + 2) + 4 * (2 * OUT_C * N + IN_C * N + OUT_C * IN_C)

F32 = mybir.dt.float32
BF16 = mybir.dt.bfloat16
U32 = mybir.dt.uint32
U8 = mybir.dt.uint8
E4M3 = mybir.dt.float8_e4m3fn_x4
E5M2 = mybir.dt.float8_e5m2_x4
ALU = mybir.AluOpType
ACT = mybir.ActivationFunctionType

P = 128
PACK = 4
PASSES = OUT_C // (P * PACK)
HALF = N // 2
SUM_BANKS = 3
CHUNKS = [(0, 1), (1, 1), (2, 2), (4, 2), (6, 2)]


def tile_mdlstmcellweights_pb_v_kernel(
    tc, x, h_prev_dim0, h_prev_dim1, ct0, ct1, w_io, w_ho, b_o, weighted_sum, o_dim0, o_dim1, grad_out, out_0, out_1
):
    nc = tc.nc

    def slabs_of(hbm, first, count):
        g, j = divmod(first, PACK)
        return hbm.rearrange("(g p j) n -> p g j n", p=P, j=PACK)[:, g, j : j + count, :]

    def by_pair(ap):
        return ap.rearrange("p (k u e) -> p u k e", u=2, e=2)

    chunk_of = {first + jj: (i, jj) for i, (first, count) in enumerate(CHUNKS) for jj in range(count)}

    with ExitStack() as ctx:
        sb = ctx.enter_context(tc.tile_pool(name="sb", bufs=1))
        ps = ctx.enter_context(tc.psum_pool(name="ps", bufs=1))
        ctx.enter_context(tc.manual_schedule())

        ident = sb.tile([P, P], F32, name="ident")
        make_identity(nc, ident[:])

        gates, cells, grads = [], [], []
        for i, (first, count) in enumerate(CHUNKS):
            gates.append(sb.tile([P, 2, count, N], F32, name="gates%d" % i))
            cells.append([sb.tile([P, count, N], BF16, name="cell%d_%d" % (i, d)) for d in range(2)])
            grads.append(sb.tile([P, count, N], BF16, name="grad%d" % i))
        ws = sb.tile([P, 2], BF16, name="ws")
        x_raw = sb.tile([P, PACK, N], BF16, name="x_raw")
        w_raw = [sb.tile([P, PACK, IN_C], BF16, name="w_raw%d" % g) for g in range(PASSES)]

        def load_gate(i, d):
            nc.sync.dma_start(out=gates[i][:, d], in_=slabs_of((o_dim0, o_dim1)[d], *CHUNKS[i]))

        def load_cell(i, d):
            nc.sync.dma_start(out=cells[i][d][:], in_=slabs_of((ct0, ct1)[d], *CHUNKS[i]))

        def load_grad(i):
            nc.sync.dma_start(out=grads[i][:], in_=slabs_of(grad_out, *CHUNKS[i]))

        def load_w(g):
            nc.sync.dma_start(out=w_raw[g][:], in_=slabs_of(w_io, g * PACK, PACK))

        nc.scalar.dma_start(out=ws[:], in_=weighted_sum.partition_broadcast(P))
        for i in range(2):
            for d in range(2):
                load_gate(i, d)
                load_cell(i, d)
            load_grad(i)
        load_gate(2, 0)
        load_cell(2, 0)
        load_cell(2, 1)
        load_grad(2)
        load_cell(3, 0)
        load_gate(2, 1)
        load_cell(3, 1)
        nc.sync.dma_start(out=x_raw[:], in_=x.rearrange("(p a) n -> p a n", a=PACK))
        load_gate(3, 0)
        load_w(0)
        load_grad(3)
        load_cell(4, 0)
        load_gate(3, 1)
        load_cell(4, 1)
        load_gate(4, 0)
        load_w(1)
        load_grad(4)
        load_gate(4, 1)

        tanhs, slopes, terms, sums = {}, {}, {}, {}
        grad_bank, grad_pos, dz_pos, pos_mx = {}, {}, {}, {}
        back, dz_chan, chan_mx = {}, {}, {}
        x_bank, w_packed, w_mx, dw_acc, dx_acc = {}, {}, {}, {}, {}
        x_packed = sb.tile([P, IN_C * PACK], BF16, name="x_packed", align_bytes=64)

        def mx_tiles(name, width):
            codes = sb.tile([P, width], U32, name=name + "_codes", align_bytes=64)
            scales = sb.tile([P, width], U8, name=name + "_scales", align_bytes=64)
            return codes, scales

        x_mx = mx_tiles("x", IN_C)

        ws_neg = sb.tile([P, 2], F32, name="ws_neg")
        nc.vector.tensor_scalar_mul(ws_neg[:], ws[:], -1.0)

        def quantize(mx, cols, src, fmt):
            nc.vector.quantize_mx(out=mx[0][:, cols].bitcast(fmt), scales=mx[1][:, cols], in_=src)

        def matmul_mx(acc, lhs, cols, lhs_fmt, rhs, rhs_fmt, start, stop):
            nc.tensor.matmul_mx(
                out=acc[:],
                lhsT=lhs[0][:, cols].bitcast(lhs_fmt),
                lhsT_scale=lhs[1][:, cols],
                rhs=rhs[0][:].bitcast(rhs_fmt),
                rhs_scale=rhs[1][:],
                start=start,
                stop=stop,
            )

        def turn_pairs(bank, pairs, row, u):
            nc.tensor.transpose(bank, pairs[:, row * HALF + u : (row + 1) * HALF : 2], ident[:])


        def turn_x():
            pairs = x_raw[:].rearrange("p a n -> p (a n)").bitcast(F32)
            for h in range(2):
                x_bank[h] = ps.tile([P, 4, P], F32, name="x_bank%d" % h, tag="dw", bufs=2)
                for a in range(2):
                    for u in range(2):
                        turn_pairs(x_bank[h][:, 2 * a + u, :], pairs, 2 * h + a, u)

        def pack_x():
            for h in range(2):
                nc.scalar.copy(
                    out=x_packed[:].bitcast(F32).rearrange("m (p h k) -> m h p k", h=2, k=4)[:, h],
                    in_=x_bank[h][:].rearrange("m k p -> m p k"),
                )

        def pack_w(g, half):
            if half == 0:
                w_packed[g] = sb.tile([P, IN_C * PACK], BF16, name="w_packed%d" % g, align_bytes=64)
            fours = slice(half * HALF // 4, (half + 1) * HALF // 4)
            nc.scalar.copy(
                out=w_packed[g][:].rearrange("p (k i j) -> p k j i", i=4, j=PACK)[:, fours],
                in_=w_raw[g][:].rearrange("p j (k i) -> p k j i", i=4)[:, fours],
            )

        def quantize_w(g, c0, c1):
            if c0 == 0:
                w_mx[g] = mx_tiles("w%d" % g, IN_C)
            quantize(w_mx[g], slice(c0, c1), w_packed[g][:, c0 * PACK : c1 * PACK], E4M3)


        def tanh_of(i, d):
            count = CHUNKS[i][1]
            tanhs[i, d] = sb.tile([P, 2, count * HALF], F32, name="tanh%d_%d" % (i, d))
            nc.scalar.activation(
                out=tanhs[i, d][:].rearrange("p u (k e) -> p u k e", e=2),
                in_=by_pair(cells[i][d][:].rearrange("p j n -> p (j n)")),
                func=ACT.Tanh,
            )

        def turn_grad(i):
            count = CHUNKS[i][1]
            pairs = grads[i][:].rearrange("p j n -> p (j n)").bitcast(F32)
            grad_bank[i] = ps.tile([P, count * 2, P], F32, name="grad_bank%d" % i, tag="grad")
            for jj in range(count):
                for u in range(2):
                    turn_pairs(grad_bank[i][:, 2 * jj + u, :], pairs, jj, u)

        def pack_grad(i):
            count = CHUNKS[i][1]
            grad_pos[i] = sb.tile([P, count * N], BF16, name="grad_t%d" % i)
            nc.scalar.copy(
                out=grad_pos[i][:].bitcast(F32).rearrange("m (j p u) -> m j p u", j=count, u=2),
                in_=grad_bank[i][:].rearrange("m (j u) p -> m j p u", u=2),
            )

        def gate_slope(i, d):
            width = CHUNKS[i][1] * N
            if d == 0:
                slopes[i] = sb.tile([P, 2 * width], F32, name="slope%d" % i, tag="slope", bufs=2)
            o = gates[i][:, d : d + 1].rearrange("p d j n -> p (d j n)")
            nc.vector.scalar_tensor_tensor(
                out=slopes[i][:, d * width : (d + 1) * width], in0=o, scalar=1.0, in1=o, op0=ALU.subtract, op1=ALU.mult
            )

        def direction_term(i, d, jj0, jj1):
            first, count = CHUNKS[i]
            if jj0 == 0:
                terms[i, d] = sb.tile([P, 2, count * HALF], F32, name="term%d_%d" % (i, d), tag="term", bufs=2)
            term = terms[i, d]
            ks = slice(jj0 * P, jj1 * P)
            for u in range(2):
                nc.vector.scalar_tensor_tensor(
                    out=term[:, u, :].rearrange("p (k e) -> p k e", e=2)[:, ks],
                    in0=tanhs[i, d][:, u, :].rearrange("p (k e) -> p k e", e=2)[:, ks],
                    scalar=ws_neg[:, d : d + 1],
                    in1=by_pair(slopes[i][:, d * count * N : (d + 1) * count * N])[:, u, ks],
                    op0=ALU.mult,
                    op1=ALU.mult,
                )
                for jj in range(jj0, jj1):
                    s = first + jj
                    if d == 0 and u == 0:
                        sums[s] = ps.tile([P, PACK, P], F32, name="sum%d" % s, tag="sum%d" % (s % SUM_BANKS))
                    for e in range(2):
                        t = 2 * u + e
                        nc.tensor.matmul(
                            sums[s][:, t, :],
                            lhsT=term[:, u, jj * HALF + e : (jj + 1) * HALF : 2],
                            rhs=ident[:],
                            is_transpose=True,
                            start=(d == 0 and t == 0),
                            stop=(d == 1 and t == PACK - 1),
                        )

        def round_dz(i):
            first, count = CHUNKS[i]
            dz_pos[i] = sb.tile([P, count * N], BF16, name="dz_pos%d" % i, align_bytes=64)
            pairs = dz_pos[i][:].bitcast(F32)
            for jj in range(count):
                cols = slice(jj * N, (jj + 1) * N)
                nc.vector.tensor_tensor(
                    out=dz_pos[i][:, cols].rearrange("m (k r t) -> m k t r", r=2, t=PACK),
                    in0=sums[first + jj][:].rearrange("m t (k r) -> m k t r", r=2),
                    in1=grad_pos[i][:, cols].rearrange("m (k r t) -> m k t r", r=2, t=PACK),
                    op=ALU.mult,
                )
                g, j = divmod(first + jj, PACK)
                for u in range(2):
                    if j == 0:
                        back[g, u] = ps.tile([P, PACK, P], F32, name="back%d_%d" % (g, u), tag="back%d" % u)
                    turn_pairs(back[g, u][:, j, :], pairs, jj, u)

        def quantize_pos(i):
            width = CHUNKS[i][1] * P
            pos_mx[i] = mx_tiles("pos%d" % i, width)
            quantize(pos_mx[i], slice(0, width), dz_pos[i][:], E5M2)

        def pack_chan(g, u, copy):
            dz_chan[g, u] = sb.tile([P, HALF * PACK], BF16, name="dz_chan%d_%d" % (g, u), align_bytes=64)
            copy(
                out=dz_chan[g, u][:].rearrange("p (k j) -> p k j", j=PACK),
                in_=back[g, u][:].rearrange("p j m -> p (j m)").bitcast(BF16).rearrange("p (j k) -> p k j", j=PACK),
            )

        def quantize_chan(g, u):
            if g not in chan_mx:
                chan_mx[g] = mx_tiles("chan%d" % g, N)
            quantize(chan_mx[g], slice(u * HALF, (u + 1) * HALF), dz_chan[g, u][:], E5M2)


        def dw_matmul(s):
            i, jj = chunk_of[s]
            dw_acc[s] = ps.tile([P, IN_C], F32, name="dw_acc%d" % s, tag="dw", bufs=2)
            matmul_mx(dw_acc[s], pos_mx[i], slice(jj * P, (jj + 1) * P), E5M2, x_mx, E4M3, True, True)

        def dw_store(s):
            res = sb.tile([P, 1, IN_C], F32, name="dw%d" % s)
            nc.scalar.copy(out=res[:, 0, :], in_=dw_acc[s][:])
            nc.sync.dma_start(out=slabs_of(out_1, s, 1), in_=res[:])

        dx_banks = ["sum%d" % (5 % SUM_BANKS), "grad", "sum%d" % (6 % SUM_BANKS), "sum%d" % (7 % SUM_BANKS)]

        def dx_matmul(a, g):
            if g == 0:
                dx_acc[a] = ps.tile([P, N], F32, name="dx_acc%d" % a, tag=dx_banks[a])
            matmul_mx(dx_acc[a], w_mx[g], slice(a * P, (a + 1) * P), E4M3, chan_mx[g], E5M2, g == 0, g == PASSES - 1)

        def dx_store(a, copy):
            res = sb.tile([P, N], F32, name="dx%d" % a)
            copy(
                out=res[:].rearrange("p (m u e) -> p m u e", u=2, e=2),
                in_=dx_acc[a][:].rearrange("p (u m e) -> p m u e", u=2, e=2),
            )
            nc.sync.dma_start(out=out_0[a * P : (a + 1) * P, :], in_=res[:])


        for d in range(2):
            tanh_of(0, d)
            gate_slope(0, d)
        turn_grad(0)
        pack_grad(0)
        for d in range(2):
            direction_term(0, d, 0, 1)
        for d in range(2):
            tanh_of(1, d)

        turn_grad(1)
        pack_grad(1)
        for d in range(2):
            gate_slope(1, d)
        round_dz(0)
        direction_term(1, 0, 0, 1)
        quantize_pos(0)
        direction_term(1, 1, 0, 1)
        for d in range(2):
            tanh_of(2, d)

        turn_grad(2)
        pack_grad(2)
        for d in range(2):
            tanh_of(3, d)
        gate_slope(2, 0)
        round_dz(1)
        direction_term(2, 0, 0, 2)
        turn_x()
        pack_x()
        gate_slope(2, 1)
        quantize_pos(1)
        direction_term(2, 1, 0, 2)
        for half in range(2):
            pack_w(0, half)

        turn_grad(3)
        pack_grad(3)
        gate_slope(3, 0)
        quantize(x_mx, slice(0, IN_C), x_packed[:], E4M3)
        for s in (0, 1):
            dw_matmul(s)
        round_dz(2)
        tanh_of(4, 0)
        for s in (0, 1):
            dw_store(s)
        for u in range(2):
            pack_chan(0, u, nc.scalar.copy)
        direction_term(3, 0, 0, 2)
        quantize_pos(2)
        for s in (2, 3):
            dw_matmul(s)
        gate_slope(3, 1)
        quantize_w(0, 0, IN_C)
        direction_term(3, 1, 0, 2)
        for s in (2, 3):
            dw_store(s)
        tanh_of(4, 1)

        turn_grad(4)
        pack_grad(4)
        gate_slope(4, 0)
        round_dz(3)
        direction_term(4, 0, 0, 2)
        quantize_pos(3)
        for s in (4, 5):
            dw_matmul(s)
        pack_w(1, 0)
        for s in (4, 5):
            dw_store(s)
        pack_w(1, 1)
        gate_slope(4, 1)
        quantize_chan(0, 0)
        for jj in range(2):
            direction_term(4, 1, jj, jj + 1)
        quantize_chan(0, 1)
        dx_matmul(0, 0)

        round_dz(4)
        dx_matmul(1, 0)
        quantize_pos(4)
        for s in (6, 7):
            dw_matmul(s)
        for a in (2, 3):
            dx_matmul(a, 0)
        pack_chan(1, 1, nc.scalar.copy)
        pack_chan(1, 0, nc.vector.tensor_copy)
        quantize_w(1, 0, HALF)
        for s in (6, 7):
            dw_store(s)
        quantize_chan(1, 1)
        quantize_chan(1, 0)
        quantize_w(1, HALF, IN_C)
        for a in range(IN_C // P):
            dx_matmul(a, 1)
            dx_store(a, (nc.vector.tensor_copy, nc.scalar.copy)[a % 2])
